import numpy as np
import ml_dtypes


def mxq(x, axis, fmt="e4m3"):
    dtype, down = {"e4m3": (ml_dtypes.float8_e4m3fn, 7), "e5m2": (ml_dtypes.float8_e5m2, 14)}[fmt]
    v = np.moveaxis(np.asarray(x, np.float32).astype(ml_dtypes.bfloat16).astype(np.float64), axis, -1)
    blocks = v.reshape(v.shape[:-1] + (-1, 32))
    amax = np.abs(blocks).max(-1, keepdims=True)
    byte = np.maximum(np.where(amax > 0, np.frexp(amax)[1] - 1 + 127, 0) - down, 1)
    scale = np.exp2(byte - 127.0)
    codes = (blocks / scale).astype(np.float32).astype(dtype).astype(np.float64)
    return np.moveaxis((codes * scale).reshape(v.shape), -1, axis)


WIDE = False


def mx_kscale(k):
    if not WIDE:
        return np.ones(k)
    levels = np.array([10, -10, 5, -5, 0])
    a = np.random.permutation(np.resize(levels, k // 512 * 4)).reshape(k // 512, 4)
    idx = np.arange(k)
    return np.exp2(a[idx // 512, idx % 128 // 32])


BF16 = ml_dtypes.bfloat16


def bf(x):
    return np.asarray(x, np.float32).astype(BF16)


def f64(x):
    return np.asarray(x).astype(np.float64)


B, C, H, W = 2, 512, 64, 64


def setup_inputs():
    t = np.exp2(np.round(np.log2(mx_kscale(C)) / 2))
    x = np.random.standard_normal((B, C, H, W)) * t[None, :, None, None]
    beta = 1.0 + 0.1 * np.random.standard_normal((1, C, 1, 1))
    gamma = (0.25 * np.eye(C) + np.exp(2.0 * np.random.standard_normal((C, C)) - 2.0) / C) / (t * t)[None, :]
    return {"x": bf(x), "beta": bf(beta), "gamma": bf(gamma.reshape(C, C, 1, 1))}


def reference(x, beta, gamma):
    x = f64(x)
    g = f64(gamma).reshape(C, C)
    xx = (x * x).reshape(B, C, H * W)
    mix = (mxq(g, 1, "e4m3") @ mxq(xx, 1, "e4m3")).reshape(B, C, H, W)
    norm = np.sqrt(f64(beta) + mix)
    return x / norm

@@ -1,0 +1,204 @@
+from contextlib import ExitStack
+
+import concourse.mybir as mybir
+from concourse.masks import make_identity
+
+F32 = mybir.dt.float32
+BF16 = mybir.dt.bfloat16
+U32 = mybir.dt.uint32
+U8 = mybir.dt.uint8
+FP8X4 = mybir.dt.float8_e4m3fn_x4
+ACT = mybir.ActivationFunctionType
+ALU = mybir.AluOpType
+
+P = 128
+PACK = 4
+BATCH = 2
+CHANNELS = 512
+PIXELS = 4096
+UNIT = 512
+HALF = 2048
+UNITS = BATCH * PIXELS // UNIT
+
+FLOPS = 2 * CHANNELS * CHANNELS * BATCH * PIXELS
+
+SCALAR_COLS = 304
+FIRST_PIECE = 256
+FIRST_SCALAR_COLS = 160
+
+X_LOADS = (
+    (0, 0, 256), (0, 256, 512), (0, 512, 1024), (0, 1024, 1536), (0, 1536, 2048),
+    (1, 0, 512), (1, 512, 1024), (1, 1024, 1536), (1, 1536, 2048),
+    (2, 0, 1024), (2, 1024, 2048),
+    (3, 0, 2048),
+)
+
+GROUPS = tuple((0, k, 1, 0, PACK) for k in range(4)) + tuple(
+    (h, 0, 4, j, 1) for h in range(1, 4) for j in range(PACK)
+)
+SQUARED_IN_STEP = ((1, 2), (3, 4), (5, 6), (7,), (8,), (9,), (10,), (11,), (12,), (13,), (14,), (15,), (), (), (), ())
+TAIL_FROM = 12
+TAIL_PIECES = 2
+LAST_PIECES = 4
+
+
+def tile_gdn_kernel(tc, x, beta, gamma, out):
+    nc = tc.nc
+    x_view = [x[b].rearrange("(p t) h w -> p t (h w)", t=PACK) for b in range(BATCH)]
+    out_view = [out[b].rearrange("(p t) h w -> p t (h w)", t=PACK) for b in range(BATCH)]
+
+    with ExitStack() as ctx:
+        keep = ctx.enter_context(tc.tile_pool(name="keep", bufs=1))
+        stage = ctx.enter_context(tc.tile_pool(name="stage", bufs=6))
+        result = ctx.enter_context(tc.tile_pool(name="result", bufs=7))
+        psum = ctx.enter_context(tc.psum_pool(name="psum", bufs=8))
+        ctx.enter_context(tc.manual_schedule())
+
+        gamma_rows = keep.tile([P, PACK * CHANNELS], BF16, name="gamma_rows")
+        nc.sync.dma_start(out=gamma_rows[:], in_=gamma.rearrange("(m j) i a b -> m (j i a b)", j=PACK))
+        beta_bf = keep.tile([P, PACK], BF16, name="beta_bf")
+        nc.sync.dma_start(out=beta_bf[:], in_=beta.rearrange("a (p j) b c -> p (a j b c)", j=PACK))
+        x_half = [keep.tile([P, PACK, HALF], BF16, name="x_half%d" % h) for h in range(4)]
+        for h, c0, c1 in X_LOADS:
+            base = (h % 2) * HALF
+            nc.sync.dma_start(out=x_half[h][:, :, c0:c1], in_=x_view[h // 2][:, :, base + c0 : base + c1])
+
+        ident = keep.tile([P, P], F32, name="ident")
+        make_identity(nc, ident[:])
+        one = keep.tile([P, 1], F32, name="one")
+        nc.vector.memset(one[:], 1.0)
+        warm = keep.tile([P, 1], F32, name="warm")
+        nc.scalar.activation(out=warm[:], in_=one[:], func=ACT.Abs_reciprocal_sqrt)
+
+        codes = [keep.tile([P, UNIT], U32, name="codes%d" % u, align_bytes=64) for u in range(UNITS)]
+        scales = [keep.tile([P, UNIT], U8, name="scales%d" % u, align_bytes=64) for u in range(UNITS)]
+        grouped = {}
+
+        def grouped_tile(u):
+            if u not in grouped:
+                grouped[u] = stage.tile([P, UNIT, PACK], BF16, name="grouped", align_bytes=64)
+            return grouped[u]
+
+        def x_cols(u, c0, c1):
+            return x_half[u // 4][:, :, (u % 4) * UNIT + c0 : (u % 4) * UNIT + c1]
+
+        def square_scalar(u, c0, c1):
+            nc.scalar.activation(
+                out=grouped_tile(u)[:, c0:c1, :].rearrange("p (c i) t -> p c t i", i=4),
+                in_=x_cols(u, c0, c1).rearrange("p t (c i) -> p c t i", i=4),
+                func=ACT.Square,
+            )
+
+        def square_vector(u, c0, c1):
+            src = x_cols(u, c0, c1).rearrange("p t w -> p w t")
+            nc.vector.tensor_tensor(out=grouped_tile(u)[:, c0:c1, :], in0=src, in1=src, op=ALU.mult)
+
+        def quantise(u):
+            nc.vector.quantize_mx(
+                out=codes[u][:].bitcast(FP8X4),
+                scales=scales[u][:],
+                in_=grouped[u][:].rearrange("p w t -> p (w t)"),
+            )
+
+        gamma_words = gamma_rows[:].bitcast(F32).rearrange("m (j q u) -> m j q u", j=PACK, u=2)
+        gamma_grouped = keep.tile([P, PACK * P * PACK], BF16, name="gamma_grouped", align_bytes=64)
+        gamma_grouped_words = gamma_grouped[:].bitcast(F32)
+        gamma_codes = keep.tile([P, PACK * P], U32, name="gamma_codes", align_bytes=64)
+        gamma_scales = keep.tile([P, PACK * P], U8, name="gamma_scales", align_bytes=64)
+        gamma_banks = []
+        for pair in range(2):
+            bank = psum.tile([P, UNIT], F32, name="bank")
+            for jj in range(2):
+                for u in range(2):
+                    col = (2 * jj + u) * P
+                    nc.tensor.transpose(bank[:, col : col + P], gamma_words[:, 2 * pair + jj, :, u], ident[:])
+            gamma_banks.append(bank)
+
+        def gamma_copy(copy, pair):
+            copy(
+                out=gamma_grouped_words[:, pair * UNIT : (pair + 1) * UNIT].rearrange(
+                    "q (jj m u) -> q jj m u", jj=2, u=2
+                ),
+                in_=gamma_banks[pair][:].rearrange("q (jj u m) -> q jj m u", jj=2, u=2),
+            )
+
+        for c0 in (0, FIRST_PIECE):
+            square_scalar(0, c0, c0 + FIRST_SCALAR_COLS)
+            square_vector(0, c0 + FIRST_SCALAR_COLS, c0 + FIRST_PIECE)
+        gamma_copy(nc.vector.tensor_copy, 0)
+        gamma_copy(nc.scalar.copy, 1)
+        beta_f = keep.tile([P, PACK], F32, name="beta_f")
+        nc.vector.tensor_copy(out=beta_f[:], in_=beta_bf[:])
+        quantise(0)
+        nc.vector.quantize_mx(out=gamma_codes[:].bitcast(FP8X4), scales=gamma_scales[:], in_=gamma_grouped[:])
+        for u in SQUARED_IN_STEP[0]:
+            square_vector(u, SCALAR_COLS, UNIT)
+
+        scaled = {}
+
+        def passes(s):
+            h, k0, nk, j0, nj = GROUPS[s]
+            banks = []
+            for j in range(j0, j0 + nj):
+                for k in range(k0, k0 + nk):
+                    u = 4 * h + k
+                    bank = psum.tile([P, UNIT], F32, name="bank")
+                    nc.tensor.matmul_mx(
+                        out=bank[:],
+                        lhsT=gamma_codes[:, j * P : (j + 1) * P].bitcast(FP8X4),
+                        lhsT_scale=gamma_scales[:, j * P : (j + 1) * P],
+                        rhs=codes[u][:].bitcast(FP8X4),
+                        rhs_scale=scales[u][:],
+                        start=True,
+                        stop=True,
+                    )
+                    banks.append(bank)
+            return banks
+
+        def inverse_roots(s, banks):
+            h, k0, nk, j0, nj = GROUPS[s]
+            scaled[s] = result.tile([P, nj, nk * UNIT], F32, name="scaled")
+            for jj in range(nj):
+                for kk in range(nk):
+                    nc.scalar.activation(
+                        out=scaled[s][:, jj, kk * UNIT : (kk + 1) * UNIT],
+                        in_=banks[jj * nk + kk][:],
+                        func=ACT.Abs_reciprocal_sqrt,
+                        bias=beta_f[:, j0 + jj : j0 + jj + 1],
+                        scale=1.0,
+                    )
+
+        def finish(s, pieces):
+            h, k0, nk, j0, nj = GROUPS[s]
+            width = nk * UNIT // pieces
+            for i in range(pieces):
+                a = i * width
+                part = scaled[s][:, :, a : a + width]
+                col = k0 * UNIT + a
+                nc.vector.tensor_tensor(
+                    out=part, in0=part, in1=x_half[h][:, j0 : j0 + nj, col : col + width], op=ALU.mult
+                )
+                base = (h % 2) * HALF + col
+                nc.sync.dma_start(out=out_view[h // 2][:, j0 : j0 + nj, base : base + width], in_=part)
+
+        steps = len(GROUPS)
+        for s in range(steps):
+            banks = passes(s)
+            units = SQUARED_IN_STEP[s]
+            for u in units[:1]:
+                square_scalar(u, 0, SCALAR_COLS)
+            inverse_roots(s, banks)
+            for u in units[1:]:
+                square_scalar(u, 0, SCALAR_COLS)
+            if s + 1 < steps:
+                for u in SQUARED_IN_STEP[s + 1]:
+                    square_vector(u, SCALAR_COLS, UNIT)
+            if s > 0:
+                for u in SQUARED_IN_STEP[s - 1][1:]:
+                    quantise(u)
+            if 0 < s <= TAIL_FROM:
+                finish(s - 1, 1)
+            if s >= TAIL_FROM:
+                finish(s, LAST_PIECES if s == steps - 1 else TAIL_PIECES)
+            for u in units[:1]:
+                quantise(u)

@@ -90,8 +90,10 @@ def tile_gdn_kernel(tc, x, beta, gamma, out):
             )
 
         def square_vector(u, c0, c1):
-            src = x_cols(u, c0, c1).rearrange("p t w -> p w t")
-            nc.vector.tensor_tensor(out=grouped_tile(u)[:, c0:c1, :], in0=src, in1=src, op=ALU.mult)
+            src = x_cols(u, c0, c1).rearrange("p t (c i) -> p c t i", i=4)
+            nc.vector.tensor_tensor(
+                out=grouped_tile(u)[:, c0:c1, :].rearrange("p (c i) t -> p c t i", i=4), in0=src, in1=src, op=ALU.mult
+            )
 
         def quantise(u):
             nc.vector.quantize_mx(

@@ -22,7 +22,7 @@ UNITS = BATCH * PIXELS // UNIT
 
 FLOPS = 2 * CHANNELS * CHANNELS * BATCH * PIXELS
 
-SCALAR_COLS = 304
+SCALAR_COLS = 256
 FIRST_PIECE = 256
 FIRST_SCALAR_COLS = 160
 
@@ -37,6 +37,7 @@ GROUPS = tuple((0, k, 1, 0, PACK) for k in range(4)) + tuple(
     (h, 0, 4, j, 1) for h in range(1, 4) for j in range(PACK)
 )
 SQUARED_IN_STEP = ((1, 2), (3, 4), (5, 6), (7,), (8,), (9,), (10,), (11,), (12,), (13,), (14,), (15,), (), (), (), ())
+ASSISTED = 12
 TAIL_FROM = 12
 TAIL_PIECES = 2
 LAST_PIECES = 4
@@ -51,7 +52,7 @@ def tile_gdn_kernel(tc, x, beta, gamma, out):
         keep = ctx.enter_context(tc.tile_pool(name="keep", bufs=1))
         stage = ctx.enter_context(tc.tile_pool(name="stage", bufs=6))
         result = ctx.enter_context(tc.tile_pool(name="result", bufs=7))
-        psum = ctx.enter_context(tc.psum_pool(name="psum", bufs=8))
+        psum = ctx.enter_context(tc.psum_pool(name="psum", bufs=4))
         ctx.enter_context(tc.manual_schedule())
 
         gamma_rows = keep.tile([P, PACK * CHANNELS], BF16, name="gamma_rows")
@@ -65,6 +66,8 @@ def tile_gdn_kernel(tc, x, beta, gamma, out):
 
         ident = keep.tile([P, P], F32, name="ident")
         make_identity(nc, ident[:])
+        ident_bf = keep.tile([P, P], BF16, name="ident_bf")
+        make_identity(nc, ident_bf[:])
         one = keep.tile([P, 1], F32, name="one")
         nc.vector.memset(one[:], 1.0)
         warm = keep.tile([P, 1], F32, name="warm")
@@ -137,6 +140,13 @@ def tile_gdn_kernel(tc, x, beta, gamma, out):
             square_vector(u, SCALAR_COLS, UNIT)
 
         scaled = {}
+        x_banks = {}
+
+        def block(s, i):
+            h, k0, nk, j0, nj = GROUPS[s]
+            jj, kk = divmod(i, nk)
+            col = (k0 + kk) * UNIT
+            return scaled[s][:, jj, kk * UNIT : (kk + 1) * UNIT], x_half[h][:, j0 + jj, col : col + UNIT]
 
         def passes(s):
             h, k0, nk, j0, nj = GROUPS[s]
@@ -155,6 +165,16 @@ def tile_gdn_kernel(tc, x, beta, gamma, out):
                         stop=True,
                     )
                     banks.append(bank)
+            if s < ASSISTED:
+                x_banks[s] = []
+                for i in range(2):
+                    jj, kk = divmod(i, nk)
+                    col = (k0 + kk) * UNIT
+                    x_bank = psum.tile([P, UNIT], F32, name="x_bank", bufs=4)
+                    nc.tensor.matmul(
+                        out=x_bank[:], lhsT=ident_bf[:], rhs=x_half[h][:, j0 + jj, col : col + UNIT], start=True, stop=True
+                    )
+                    x_banks[s].append(x_bank)
             return banks
 
         def inverse_roots(s, banks):
@@ -183,6 +203,18 @@ def tile_gdn_kernel(tc, x, beta, gamma, out):
                 base = (h % 2) * HALF + col
                 nc.sync.dma_start(out=out_view[h // 2][:, j0 : j0 + nj, base : base + width], in_=part)
 
+        def finish_assisted(s):
+            h, k0, nk, j0, nj = GROUPS[s]
+            part, x_part = block(s, 3)
+            nc.gpsimd.tensor_tensor(out=part, in0=part, in1=x_part, op=ALU.mult)
+            for i in range(2):
+                part, x_part = block(s, i)
+                nc.vector.tensor_tensor(out=part, in0=x_banks[s][i][:], in1=part, op=ALU.mult)
+            part, x_part = block(s, 2)
+            nc.vector.tensor_tensor(out=part, in0=part, in1=x_part, op=ALU.mult)
+            base = (h % 2) * HALF + k0 * UNIT
+            nc.sync.dma_start(out=out_view[h // 2][:, j0 : j0 + nj, base : base + nk * UNIT], in_=scaled[s][:])
+
         steps = len(GROUPS)
         for s in range(steps):
             banks = passes(s)
@@ -198,8 +230,8 @@ def tile_gdn_kernel(tc, x, beta, gamma, out):
             if s > 0:
                 for u in SQUARED_IN_STEP[s - 1][1:]:
                     quantise(u)
-            if 0 < s <= TAIL_FROM:
-                finish(s - 1, 1)
+            if 0 < s <= ASSISTED:
+                finish_assisted(s - 1)
             if s >= TAIL_FROM:
                 finish(s, LAST_PIECES if s == steps - 1 else TAIL_PIECES)
             for u in units[:1]:

@@ -27,20 +27,12 @@ FIRST_PIECE = 256
 FIRST_SCALAR_COLS = 160
 
 X_LOADS = (
-    (0, 0, 256), (0, 256, 512), (0, 512, 1024), (0, 1024, 1536), (0, 1536, 2048),
-    (1, 0, 512), (1, 512, 1024), (1, 1024, 1536), (1, 1536, 2048),
-    (2, 0, 1024), (2, 1024, 2048),
+    (0, 0, 256), (0, 256, 512), (0, 512, 1024), (0, 1024, 2048),
+    (1, 0, 1024), (1, 1024, 2048),
+    (2, 0, 2048),
     (3, 0, 2048),
 )
-
-GROUPS = tuple((0, k, 1, 0, PACK) for k in range(4)) + tuple(
-    (h, 0, 4, j, 1) for h in range(1, 4) for j in range(PACK)
-)
-SQUARED_IN_STEP = ((1, 2), (3, 4), (5, 6), (7,), (8,), (9,), (10,), (11,), (12,), (13,), (14,), (15,), (), (), (), ())
 ASSISTED = 12
-TAIL_FROM = 12
-TAIL_PIECES = 2
-LAST_PIECES = 4
 
 
 def tile_gdn_kernel(tc, x, beta, gamma, out):
@@ -50,8 +42,8 @@ def tile_gdn_kernel(tc, x, beta, gamma, out):
 
     with ExitStack() as ctx:
         keep = ctx.enter_context(tc.tile_pool(name="keep", bufs=1))
-        stage = ctx.enter_context(tc.tile_pool(name="stage", bufs=6))
-        result = ctx.enter_context(tc.tile_pool(name="result", bufs=7))
+        stage = ctx.enter_context(tc.tile_pool(name="stage", bufs=4))
+        result = ctx.enter_context(tc.tile_pool(name="result", bufs=8))
         psum = ctx.enter_context(tc.psum_pool(name="psum", bufs=4))
         ctx.enter_context(tc.manual_schedule())
 
@@ -85,18 +77,19 @@ def tile_gdn_kernel(tc, x, beta, gamma, out):
         def x_cols(u, c0, c1):
             return x_half[u // 4][:, :, (u % 4) * UNIT + c0 : (u % 4) * UNIT + c1]
 
-        def square_scalar(u, c0, c1):
-            nc.scalar.activation(
-                out=grouped_tile(u)[:, c0:c1, :].rearrange("p (c i) t -> p c t i", i=4),
-                in_=x_cols(u, c0, c1).rearrange("p t (c i) -> p c t i", i=4),
-                func=ACT.Square,
+        def square_views(u, c0, c1):
+            return (
+                grouped_tile(u)[:, c0:c1, :].rearrange("p (c i) t -> p c t i", i=4),
+                x_cols(u, c0, c1).rearrange("p t (c i) -> p c t i", i=4),
             )
 
+        def square_scalar(u, c0, c1):
+            dst, src = square_views(u, c0, c1)
+            nc.scalar.activation(out=dst, in_=src, func=ACT.Square)
+
         def square_vector(u, c0, c1):
-            src = x_cols(u, c0, c1).rearrange("p t (c i) -> p c t i", i=4)
-            nc.vector.tensor_tensor(
-                out=grouped_tile(u)[:, c0:c1, :].rearrange("p (c i) t -> p c t i", i=4), in0=src, in1=src, op=ALU.mult
-            )
+            dst, src = square_views(u, c0, c1)
+            nc.vector.tensor_tensor(out=dst, in0=src, in1=src, op=ALU.mult)
 
         def quantise(u):
             nc.vector.quantize_mx(
@@ -127,6 +120,13 @@ def tile_gdn_kernel(tc, x, beta, gamma, out):
                 in_=gamma_banks[pair][:].rearrange("q (jj u m) -> q jj m u", jj=2, u=2),
             )
 
+        def gamma_quantise(pair):
+            nc.vector.quantize_mx(
+                out=gamma_codes[:, pair * 2 * P : (pair + 1) * 2 * P].bitcast(FP8X4),
+                scales=gamma_scales[:, pair * 2 * P : (pair + 1) * 2 * P],
+                in_=gamma_grouped[:, pair * 2 * P * PACK : (pair + 1) * 2 * P * PACK],
+            )
+
         for c0 in (0, FIRST_PIECE):
             square_scalar(0, c0, c0 + FIRST_SCALAR_COLS)
             square_vector(0, c0 + FIRST_SCALAR_COLS, c0 + FIRST_PIECE)
@@ -134,105 +134,75 @@ def tile_gdn_kernel(tc, x, beta, gamma, out):
         gamma_copy(nc.scalar.copy, 1)
         beta_f = keep.tile([P, PACK], F32, name="beta_f")
         nc.vector.tensor_copy(out=beta_f[:], in_=beta_bf[:])
+        gamma_quantise(0)
         quantise(0)
-        nc.vector.quantize_mx(out=gamma_codes[:].bitcast(FP8X4), scales=gamma_scales[:], in_=gamma_grouped[:])
-        for u in SQUARED_IN_STEP[0]:
-            square_vector(u, SCALAR_COLS, UNIT)
+        gamma_quantise(1)
+        square_vector(1, SCALAR_COLS, UNIT)
 
         scaled = {}
         x_banks = {}
 
-        def block(s, i):
-            h, k0, nk, j0, nj = GROUPS[s]
-            jj, kk = divmod(i, nk)
-            col = (k0 + kk) * UNIT
-            return scaled[s][:, jj, kk * UNIT : (kk + 1) * UNIT], x_half[h][:, j0 + jj, col : col + UNIT]
+        def x_row(u, j):
+            return x_half[u // 4][:, j, (u % 4) * UNIT : (u % 4 + 1) * UNIT]
 
-        def passes(s):
-            h, k0, nk, j0, nj = GROUPS[s]
+        def out_cols(u):
+            return out_view[u // 8][:, :, (u % 8) * UNIT : (u % 8 + 1) * UNIT]
+
+        def passes(u):
             banks = []
-            for j in range(j0, j0 + nj):
-                for k in range(k0, k0 + nk):
-                    u = 4 * h + k
-                    bank = psum.tile([P, UNIT], F32, name="bank")
-                    nc.tensor.matmul_mx(
-                        out=bank[:],
-                        lhsT=gamma_codes[:, j * P : (j + 1) * P].bitcast(FP8X4),
-                        lhsT_scale=gamma_scales[:, j * P : (j + 1) * P],
-                        rhs=codes[u][:].bitcast(FP8X4),
-                        rhs_scale=scales[u][:],
-                        start=True,
-                        stop=True,
-                    )
-                    banks.append(bank)
-            if s < ASSISTED:
-                x_banks[s] = []
-                for i in range(2):
-                    jj, kk = divmod(i, nk)
-                    col = (k0 + kk) * UNIT
-                    x_bank = psum.tile([P, UNIT], F32, name="x_bank", bufs=4)
-                    nc.tensor.matmul(
-                        out=x_bank[:], lhsT=ident_bf[:], rhs=x_half[h][:, j0 + jj, col : col + UNIT], start=True, stop=True
-                    )
-                    x_banks[s].append(x_bank)
+            for j in range(PACK):
+                bank = psum.tile([P, UNIT], F32, name="bank")
+                nc.tensor.matmul_mx(
+                    out=bank[:],
+                    lhsT=gamma_codes[:, j * P : (j + 1) * P].bitcast(FP8X4),
+                    lhsT_scale=gamma_scales[:, j * P : (j + 1) * P],
+                    rhs=codes[u][:].bitcast(FP8X4),
+                    rhs_scale=scales[u][:],
+                    start=True,
+                    stop=True,
+                )
+                banks.append(bank)
+            if u < ASSISTED:
+                x_banks[u] = []
+                for j in range(2):
+                    x_bank = psum.tile([P, UNIT], F32, name="x_bank")
+                    nc.tensor.matmul(out=x_bank[:], lhsT=ident_bf[:], rhs=x_row(u, j), start=True, stop=True)
+                    x_banks[u].append(x_bank)
             return banks
 
-        def inverse_roots(s, banks):
-            h, k0, nk, j0, nj = GROUPS[s]
-            scaled[s] = result.tile([P, nj, nk * UNIT], F32, name="scaled")
-            for jj in range(nj):
-                for kk in range(nk):
-                    nc.scalar.activation(
-                        out=scaled[s][:, jj, kk * UNIT : (kk + 1) * UNIT],
-                        in_=banks[jj * nk + kk][:],
-                        func=ACT.Abs_reciprocal_sqrt,
-                        bias=beta_f[:, j0 + jj : j0 + jj + 1],
-                        scale=1.0,
-                    )
-
-        def finish(s, pieces):
-            h, k0, nk, j0, nj = GROUPS[s]
-            width = nk * UNIT // pieces
-            for i in range(pieces):
-                a = i * width
-                part = scaled[s][:, :, a : a + width]
-                col = k0 * UNIT + a
-                nc.vector.tensor_tensor(
-                    out=part, in0=part, in1=x_half[h][:, j0 : j0 + nj, col : col + width], op=ALU.mult
+        def inverse_roots(u, banks):
+            scaled[u] = result.tile([P, PACK, UNIT], F32, name="scaled")
+            for j in range(PACK):
+                nc.scalar.activation(
+                    out=scaled[u][:, j, :],
+                    in_=banks[j][:],
+                    func=ACT.Abs_reciprocal_sqrt,
+                    bias=beta_f[:, j : j + 1],
+                    scale=1.0,
                 )
-                base = (h % 2) * HALF + col
-                nc.sync.dma_start(out=out_view[h // 2][:, j0 : j0 + nj, base : base + width], in_=part)
 
-        def finish_assisted(s):
-            h, k0, nk, j0, nj = GROUPS[s]
-            part, x_part = block(s, 3)
-            nc.gpsimd.tensor_tensor(out=part, in0=part, in1=x_part, op=ALU.mult)
-            for i in range(2):
-                part, x_part = block(s, i)
-                nc.vector.tensor_tensor(out=part, in0=x_banks[s][i][:], in1=part, op=ALU.mult)
-            part, x_part = block(s, 2)
-            nc.vector.tensor_tensor(out=part, in0=part, in1=x_part, op=ALU.mult)
-            base = (h % 2) * HALF + k0 * UNIT
-            nc.sync.dma_start(out=out_view[h // 2][:, j0 : j0 + nj, base : base + nk * UNIT], in_=scaled[s][:])
+        def finish_assisted(u):
+            nc.gpsimd.tensor_tensor(out=scaled[u][:, 3, :], in0=scaled[u][:, 3, :], in1=x_row(u, 3), op=ALU.mult)
+            for j in range(2):
+                nc.vector.tensor_tensor(out=scaled[u][:, j, :], in0=x_banks[u][j][:], in1=scaled[u][:, j, :], op=ALU.mult)
+            nc.vector.tensor_tensor(out=scaled[u][:, 2, :], in0=scaled[u][:, 2, :], in1=x_row(u, 2), op=ALU.mult)
+            nc.sync.dma_start(out=out_cols(u), in_=scaled[u][:])
 
-        steps = len(GROUPS)
-        for s in range(steps):
-            banks = passes(s)
-            units = SQUARED_IN_STEP[s]
-            for u in units[:1]:
-                square_scalar(u, 0, SCALAR_COLS)
-            inverse_roots(s, banks)
-            for u in units[1:]:
-                square_scalar(u, 0, SCALAR_COLS)
-            if s + 1 < steps:
-                for u in SQUARED_IN_STEP[s + 1]:
-                    square_vector(u, SCALAR_COLS, UNIT)
-            if s > 0:
-                for u in SQUARED_IN_STEP[s - 1][1:]:
-                    quantise(u)
-            if 0 < s <= ASSISTED:
-                finish_assisted(s - 1)
-            if s >= TAIL_FROM:
-                finish(s, LAST_PIECES if s == steps - 1 else TAIL_PIECES)
-            for u in units[:1]:
-                quantise(u)
+        def finish_by_rows(u):
+            for j in range(PACK):
+                nc.vector.tensor_tensor(out=scaled[u][:, j, :], in0=scaled[u][:, j, :], in1=x_row(u, j), op=ALU.mult)
+                nc.sync.dma_start(out=out_cols(u)[:, j, :], in_=scaled[u][:, j, :])
+
+        for u in range(UNITS):
+            banks = passes(u)
+            if u + 1 < UNITS:
+                square_scalar(u + 1, 0, SCALAR_COLS)
+            inverse_roots(u, banks)
+            if u + 2 < UNITS:
+                square_vector(u + 2, SCALAR_COLS, UNIT)
+            if 0 < u <= ASSISTED:
+                finish_assisted(u - 1)
+            if u + 1 < UNITS:
+                quantise(u + 1)
+            if u >= ASSISTED:
+                finish_by_rows(u)

@@ -22,7 +22,7 @@ UNITS = BATCH * PIXELS // UNIT
 
 FLOPS = 2 * CHANNELS * CHANNELS * BATCH * PIXELS
 
-SCALAR_COLS = 256
+SCALAR_COLS = 272
 FIRST_PIECE = 256
 FIRST_SCALAR_COLS = 160
 
@@ -33,6 +33,7 @@ X_LOADS = (
     (3, 0, 2048),
 )
 ASSISTED = 12
+VECTOR_COLS = 320
 
 
 def tile_gdn_kernel(tc, x, beta, gamma, out):
@@ -182,10 +183,12 @@ def tile_gdn_kernel(tc, x, beta, gamma, out):
                 )
 
         def finish_assisted(u):
-            nc.gpsimd.tensor_tensor(out=scaled[u][:, 3, :], in0=scaled[u][:, 3, :], in1=x_row(u, 3), op=ALU.mult)
+            rest = scaled[u][:, 2:PACK, VECTOR_COLS:UNIT]
+            nc.gpsimd.tensor_tensor(out=rest, in0=rest, in1=x_cols(u, VECTOR_COLS, UNIT)[:, 2:PACK, :], op=ALU.mult)
             for j in range(2):
                 nc.vector.tensor_tensor(out=scaled[u][:, j, :], in0=x_banks[u][j][:], in1=scaled[u][:, j, :], op=ALU.mult)
-            nc.vector.tensor_tensor(out=scaled[u][:, 2, :], in0=scaled[u][:, 2, :], in1=x_row(u, 2), op=ALU.mult)
+            part = scaled[u][:, 2:PACK, 0:VECTOR_COLS]
+            nc.vector.tensor_tensor(out=part, in0=part, in1=x_cols(u, 0, VECTOR_COLS)[:, 2:PACK, :], op=ALU.mult)
             nc.sync.dma_start(out=out_cols(u), in_=scaled[u][:])
 
         def finish_by_rows(u):

@@ -45,7 +45,7 @@ def tile_gdn_kernel(tc, x, beta, gamma, out):
         keep = ctx.enter_context(tc.tile_pool(name="keep", bufs=1))
         stage = ctx.enter_context(tc.tile_pool(name="stage", bufs=4))
         result = ctx.enter_context(tc.tile_pool(name="result", bufs=8))
-        psum = ctx.enter_context(tc.psum_pool(name="psum", bufs=4))
+        psum = ctx.enter_context(tc.psum_pool(name="psum", bufs=6))
         ctx.enter_context(tc.manual_schedule())
 
         gamma_rows = keep.tile([P, PACK * CHANNELS], BF16, name="gamma_rows")
@@ -164,11 +164,9 @@ def tile_gdn_kernel(tc, x, beta, gamma, out):
                 )
                 banks.append(bank)
             if u < ASSISTED:
-                x_banks[u] = []
+                x_banks[u] = psum.tile([P, 2, UNIT], BF16, name="x_bank", bufs=2)
                 for j in range(2):
-                    x_bank = psum.tile([P, UNIT], F32, name="x_bank")
-                    nc.tensor.matmul(out=x_bank[:], lhsT=ident_bf[:], rhs=x_row(u, j), start=True, stop=True)
-                    x_banks[u].append(x_bank)
+                    nc.tensor.matmul(out=x_banks[u][:, j, :], lhsT=ident_bf[:], rhs=x_row(u, j), start=True, stop=True)
             return banks
 
         def inverse_roots(u, banks):
@@ -185,8 +183,7 @@ def tile_gdn_kernel(tc, x, beta, gamma, out):
         def finish_assisted(u):
             rest = scaled[u][:, 2:PACK, VECTOR_COLS:UNIT]
             nc.gpsimd.tensor_tensor(out=rest, in0=rest, in1=x_cols(u, VECTOR_COLS, UNIT)[:, 2:PACK, :], op=ALU.mult)
-            for j in range(2):
-                nc.vector.tensor_tensor(out=scaled[u][:, j, :], in0=x_banks[u][j][:], in1=scaled[u][:, j, :], op=ALU.mult)
+            nc.vector.tensor_tensor(out=scaled[u][:, 0:2, :], in0=x_banks[u][:], in1=scaled[u][:, 0:2, :], op=ALU.mult)
             part = scaled[u][:, 2:PACK, 0:VECTOR_COLS]
             nc.vector.tensor_tensor(out=part, in0=part, in1=x_cols(u, 0, VECTOR_COLS)[:, 2:PACK, :], op=ALU.mult)
             nc.sync.dma_start(out=out_cols(u), in_=scaled[u][:])

@@ -17,22 +17,21 @@ BATCH = 2
 CHANNELS = 512
 PIXELS = 4096
 UNIT = 512
-HALF = 2048
 UNITS = BATCH * PIXELS // UNIT
 
 FLOPS = 2 * CHANNELS * CHANNELS * BATCH * PIXELS
 
-SCALAR_COLS = 272
+X_WIDTHS = (256, 256, 512, 512, 512, 512, 512, 1024, 2048, 2048)
+GAMMA_AFTER = 5
+BETA_AFTER = 6
+
+LEAD = 5
+SCALAR_COLS = 280
+HEAD_SCALAR_COLS = 304
 FIRST_PIECE = 256
 FIRST_SCALAR_COLS = 160
-
-X_LOADS = (
-    (0, 0, 256), (0, 256, 512), (0, 512, 1024), (0, 1024, 2048),
-    (1, 0, 1024), (1, 1024, 2048),
-    (2, 0, 2048),
-    (3, 0, 2048),
-)
-ASSISTED = 12
+FIRST_ASSISTED = 1
+LAST_ASSISTED = 12
 VECTOR_COLS = 320
 
 
@@ -49,13 +48,19 @@ def tile_gdn_kernel(tc, x, beta, gamma, out):
         ctx.enter_context(tc.manual_schedule())
 
         gamma_rows = keep.tile([P, PACK * CHANNELS], BF16, name="gamma_rows")
-        nc.sync.dma_start(out=gamma_rows[:], in_=gamma.rearrange("(m j) i a b -> m (j i a b)", j=PACK))
         beta_bf = keep.tile([P, PACK], BF16, name="beta_bf")
-        nc.sync.dma_start(out=beta_bf[:], in_=beta.rearrange("a (p j) b c -> p (a j b c)", j=PACK))
-        x_half = [keep.tile([P, PACK, HALF], BF16, name="x_half%d" % h) for h in range(4)]
-        for h, c0, c1 in X_LOADS:
-            base = (h % 2) * HALF
-            nc.sync.dma_start(out=x_half[h][:, :, c0:c1], in_=x_view[h // 2][:, :, base + c0 : base + c1])
+        x_tiles = []
+        start = 0
+        for i, width in enumerate(X_WIDTHS):
+            if i == GAMMA_AFTER:
+                nc.sync.dma_start(out=gamma_rows[:], in_=gamma.rearrange("(m j) i a b -> m (j i a b)", j=PACK))
+            if i == BETA_AFTER:
+                nc.sync.dma_start(out=beta_bf[:], in_=beta.rearrange("a (p j) b c -> p (a j b c)", j=PACK))
+            x_tile = keep.tile([P, PACK, width], BF16, name="x_tile%d" % i)
+            first = start % PIXELS
+            nc.sync.dma_start(out=x_tile[:], in_=x_view[start // PIXELS][:, :, first : first + width])
+            x_tiles.append((start, width, x_tile))
+            start += width
 
         ident = keep.tile([P, P], F32, name="ident")
         make_identity(nc, ident[:])
@@ -76,7 +81,10 @@ def tile_gdn_kernel(tc, x, beta, gamma, out):
             return grouped[u]
 
         def x_cols(u, c0, c1):
-            return x_half[u // 4][:, :, (u % 4) * UNIT + c0 : (u % 4) * UNIT + c1]
+            for first, width, x_tile in x_tiles:
+                if first <= u * UNIT + c0 and u * UNIT + c1 <= first + width:
+                    return x_tile[:, :, u * UNIT + c0 - first : u * UNIT + c1 - first]
+            raise ValueError("columns in two tiles")
 
         def square_views(u, c0, c1):
             return (
@@ -131,20 +139,22 @@ def tile_gdn_kernel(tc, x, beta, gamma, out):
         for c0 in (0, FIRST_PIECE):
             square_scalar(0, c0, c0 + FIRST_SCALAR_COLS)
             square_vector(0, c0 + FIRST_SCALAR_COLS, c0 + FIRST_PIECE)
+        for u in range(1, LEAD - 1):
+            square_scalar(u, 0, HEAD_SCALAR_COLS)
+            square_vector(u, HEAD_SCALAR_COLS, UNIT)
+            quantise(u - 1)
         gamma_copy(nc.vector.tensor_copy, 0)
+        square_scalar(LEAD - 1, 0, HEAD_SCALAR_COLS)
         gamma_copy(nc.scalar.copy, 1)
+        quantise(LEAD - 2)
+        gamma_quantise(0)
+        square_vector(LEAD - 1, HEAD_SCALAR_COLS, UNIT)
         beta_f = keep.tile([P, PACK], F32, name="beta_f")
         nc.vector.tensor_copy(out=beta_f[:], in_=beta_bf[:])
-        gamma_quantise(0)
-        quantise(0)
         gamma_quantise(1)
-        square_vector(1, SCALAR_COLS, UNIT)
 
         scaled = {}
         x_banks = {}
-
-        def x_row(u, j):
-            return x_half[u // 4][:, j, (u % 4) * UNIT : (u % 4 + 1) * UNIT]
 
         def out_cols(u):
             return out_view[u // 8][:, :, (u % 8) * UNIT : (u % 8 + 1) * UNIT]
@@ -163,10 +173,12 @@ def tile_gdn_kernel(tc, x, beta, gamma, out):
                     stop=True,
                 )
                 banks.append(bank)
-            if u < ASSISTED:
+            if FIRST_ASSISTED <= u <= LAST_ASSISTED:
                 x_banks[u] = psum.tile([P, 2, UNIT], BF16, name="x_bank", bufs=2)
                 for j in range(2):
-                    nc.tensor.matmul(out=x_banks[u][:, j, :], lhsT=ident_bf[:], rhs=x_row(u, j), start=True, stop=True)
+                    nc.tensor.matmul(
+                        out=x_banks[u][:, j, :], lhsT=ident_bf[:], rhs=x_cols(u, 0, UNIT)[:, 2 + j, :], start=True, stop=True
+                    )
             return banks
 
         def inverse_roots(u, banks):
@@ -181,28 +193,42 @@ def tile_gdn_kernel(tc, x, beta, gamma, out):
                 )
 
         def finish_assisted(u):
-            rest = scaled[u][:, 2:PACK, VECTOR_COLS:UNIT]
-            nc.gpsimd.tensor_tensor(out=rest, in0=rest, in1=x_cols(u, VECTOR_COLS, UNIT)[:, 2:PACK, :], op=ALU.mult)
-            nc.vector.tensor_tensor(out=scaled[u][:, 0:2, :], in0=x_banks[u][:], in1=scaled[u][:, 0:2, :], op=ALU.mult)
-            part = scaled[u][:, 2:PACK, 0:VECTOR_COLS]
-            nc.vector.tensor_tensor(out=part, in0=part, in1=x_cols(u, 0, VECTOR_COLS)[:, 2:PACK, :], op=ALU.mult)
+            part = scaled[u][:, 0:2, 0:VECTOR_COLS]
+            nc.vector.tensor_tensor(out=part, in0=part, in1=x_cols(u, 0, VECTOR_COLS)[:, 0:2, :], op=ALU.mult)
+            rest = scaled[u][:, 0:2, VECTOR_COLS:UNIT]
+            nc.gpsimd.tensor_tensor(out=rest, in0=rest, in1=x_cols(u, VECTOR_COLS, UNIT)[:, 0:2, :], op=ALU.mult)
+            nc.vector.tensor_tensor(out=scaled[u][:, 2:PACK, :], in0=x_banks[u][:], in1=scaled[u][:, 2:PACK, :], op=ALU.mult)
+            nc.sync.dma_start(out=out_cols(u)[:, 2:PACK, :], in_=scaled[u][:, 2:PACK, :])
+            nc.sync.dma_start(out=out_cols(u)[:, 0:2, :], in_=scaled[u][:, 0:2, :])
+
+        def finish_first(u):
+            for c0 in (0, FIRST_PIECE):
+                piece = scaled[u][:, :, c0 : c0 + FIRST_PIECE]
+                nc.vector.tensor_tensor(out=piece, in0=piece, in1=x_cols(u, c0, c0 + FIRST_PIECE), op=ALU.mult)
             nc.sync.dma_start(out=out_cols(u), in_=scaled[u][:])
 
-        def finish_by_rows(u):
+        def finish_by_rows(u, store_rows):
             for j in range(PACK):
-                nc.vector.tensor_tensor(out=scaled[u][:, j, :], in0=scaled[u][:, j, :], in1=x_row(u, j), op=ALU.mult)
-                nc.sync.dma_start(out=out_cols(u)[:, j, :], in_=scaled[u][:, j, :])
+                nc.vector.tensor_tensor(
+                    out=scaled[u][:, j, :], in0=scaled[u][:, j, :], in1=x_cols(u, 0, UNIT)[:, j, :], op=ALU.mult
+                )
+                if store_rows:
+                    nc.sync.dma_start(out=out_cols(u)[:, j, :], in_=scaled[u][:, j, :])
+            if not store_rows:
+                nc.sync.dma_start(out=out_cols(u), in_=scaled[u][:])
 
         for u in range(UNITS):
+            ahead = u + LEAD
             banks = passes(u)
-            if u + 1 < UNITS:
-                square_scalar(u + 1, 0, SCALAR_COLS)
             inverse_roots(u, banks)
-            if u + 2 < UNITS:
-                square_vector(u + 2, SCALAR_COLS, UNIT)
-            if 0 < u <= ASSISTED:
-                finish_assisted(u - 1)
-            if u + 1 < UNITS:
-                quantise(u + 1)
-            if u >= ASSISTED:
-                finish_by_rows(u)
+            if ahead < UNITS:
+                square_scalar(ahead, 0, SCALAR_COLS)
+                square_vector(ahead, SCALAR_COLS, UNIT)
+            if ahead - 1 < UNITS:
+                quantise(ahead - 1)
+            if u == 0:
+                finish_first(u)
+            elif FIRST_ASSISTED <= u <= LAST_ASSISTED:
+                finish_assisted(u)
+            else:
+                finish_by_rows(u, True)

@@ -25,13 +25,14 @@ X_WIDTHS = (256, 256, 512, 512, 512, 512, 512, 1024, 2048, 2048)
 GAMMA_AFTER = 5
 BETA_AFTER = 6
 
-LEAD = 5
+HEAD_UNITS = 5
+LEAD = 2
 SCALAR_COLS = 280
-HEAD_SCALAR_COLS = 304
+HEAD_SCALAR_COLS = 336
 FIRST_PIECE = 256
-FIRST_SCALAR_COLS = 160
-FIRST_ASSISTED = 1
-LAST_ASSISTED = 12
+FIRST_SCALAR_COLS = 168
+FIRST_ASSISTED = 3
+LAST_ASSISTED = 14
 VECTOR_COLS = 320
 
 
@@ -139,16 +140,16 @@ def tile_gdn_kernel(tc, x, beta, gamma, out):
         for c0 in (0, FIRST_PIECE):
             square_scalar(0, c0, c0 + FIRST_SCALAR_COLS)
             square_vector(0, c0 + FIRST_SCALAR_COLS, c0 + FIRST_PIECE)
-        for u in range(1, LEAD - 1):
+        for u in range(1, HEAD_UNITS - 1):
             square_scalar(u, 0, HEAD_SCALAR_COLS)
             square_vector(u, HEAD_SCALAR_COLS, UNIT)
             quantise(u - 1)
         gamma_copy(nc.vector.tensor_copy, 0)
-        square_scalar(LEAD - 1, 0, HEAD_SCALAR_COLS)
+        square_scalar(HEAD_UNITS - 1, 0, HEAD_SCALAR_COLS)
         gamma_copy(nc.scalar.copy, 1)
-        quantise(LEAD - 2)
+        quantise(HEAD_UNITS - 2)
         gamma_quantise(0)
-        square_vector(LEAD - 1, HEAD_SCALAR_COLS, UNIT)
+        square_vector(HEAD_UNITS - 1, HEAD_SCALAR_COLS, UNIT)
         beta_f = keep.tile([P, PACK], F32, name="beta_f")
         nc.vector.tensor_copy(out=beta_f[:], in_=beta_bf[:])
         gamma_quantise(1)
@@ -198,8 +199,11 @@ def tile_gdn_kernel(tc, x, beta, gamma, out):
             rest = scaled[u][:, 0:2, VECTOR_COLS:UNIT]
             nc.gpsimd.tensor_tensor(out=rest, in0=rest, in1=x_cols(u, VECTOR_COLS, UNIT)[:, 0:2, :], op=ALU.mult)
             nc.vector.tensor_tensor(out=scaled[u][:, 2:PACK, :], in0=x_banks[u][:], in1=scaled[u][:, 2:PACK, :], op=ALU.mult)
-            nc.sync.dma_start(out=out_cols(u)[:, 2:PACK, :], in_=scaled[u][:, 2:PACK, :])
-            nc.sync.dma_start(out=out_cols(u)[:, 0:2, :], in_=scaled[u][:, 0:2, :])
+            if u == LAST_ASSISTED:
+                nc.sync.dma_start(out=out_cols(u)[:, 2:PACK, :], in_=scaled[u][:, 2:PACK, :])
+                nc.sync.dma_start(out=out_cols(u)[:, 0:2, :], in_=scaled[u][:, 0:2, :])
+            else:
+                nc.sync.dma_start(out=out_cols(u), in_=scaled[u][:])
 
         def finish_first(u):
             for c0 in (0, FIRST_PIECE):
@@ -221,14 +225,16 @@ def tile_gdn_kernel(tc, x, beta, gamma, out):
             ahead = u + LEAD
             banks = passes(u)
             inverse_roots(u, banks)
-            if ahead < UNITS:
+            if HEAD_UNITS <= ahead < UNITS:
                 square_scalar(ahead, 0, SCALAR_COLS)
                 square_vector(ahead, SCALAR_COLS, UNIT)
-            if ahead - 1 < UNITS:
+            if u == 0:
+                quantise(HEAD_UNITS - 1)
+            if HEAD_UNITS <= ahead - 1 < UNITS:
                 quantise(ahead - 1)
             if u == 0:
                 finish_first(u)
             elif FIRST_ASSISTED <= u <= LAST_ASSISTED:
                 finish_assisted(u)
             else:
-                finish_by_rows(u, True)
+                finish_by_rows(u, u == UNITS - 1)

@@ -26,13 +26,13 @@ GAMMA_AFTER = 5
 BETA_AFTER = 6
 
 HEAD_UNITS = 5
-LEAD = 2
+VECTOR_HEAD_UNITS = 7
 SCALAR_COLS = 280
 HEAD_SCALAR_COLS = 336
 FIRST_PIECE = 256
 FIRST_SCALAR_COLS = 168
-FIRST_ASSISTED = 3
-LAST_ASSISTED = 14
+FIRST_ASSISTED = 1
+LAST_ASSISTED = 12
 VECTOR_COLS = 320
 
 
@@ -153,6 +153,9 @@ def tile_gdn_kernel(tc, x, beta, gamma, out):
         beta_f = keep.tile([P, PACK], F32, name="beta_f")
         nc.vector.tensor_copy(out=beta_f[:], in_=beta_bf[:])
         gamma_quantise(1)
+        quantise(HEAD_UNITS - 1)
+        for u in range(HEAD_UNITS, VECTOR_HEAD_UNITS):
+            square_vector(u, SCALAR_COLS, UNIT)
 
         scaled = {}
         x_banks = {}
@@ -198,11 +201,17 @@ def tile_gdn_kernel(tc, x, beta, gamma, out):
             nc.vector.tensor_tensor(out=part, in0=part, in1=x_cols(u, 0, VECTOR_COLS)[:, 0:2, :], op=ALU.mult)
             rest = scaled[u][:, 0:2, VECTOR_COLS:UNIT]
             nc.gpsimd.tensor_tensor(out=rest, in0=rest, in1=x_cols(u, VECTOR_COLS, UNIT)[:, 0:2, :], op=ALU.mult)
-            nc.vector.tensor_tensor(out=scaled[u][:, 2:PACK, :], in0=x_banks[u][:], in1=scaled[u][:, 2:PACK, :], op=ALU.mult)
             if u == LAST_ASSISTED:
-                nc.sync.dma_start(out=out_cols(u)[:, 2:PACK, :], in_=scaled[u][:, 2:PACK, :])
+                for j in range(2, PACK):
+                    nc.vector.tensor_tensor(
+                        out=scaled[u][:, j, :], in0=x_banks[u][:, j - 2, :], in1=scaled[u][:, j, :], op=ALU.mult
+                    )
+                    nc.sync.dma_start(out=out_cols(u)[:, j, :], in_=scaled[u][:, j, :])
                 nc.sync.dma_start(out=out_cols(u)[:, 0:2, :], in_=scaled[u][:, 0:2, :])
             else:
+                nc.vector.tensor_tensor(
+                    out=scaled[u][:, 2:PACK, :], in0=x_banks[u][:], in1=scaled[u][:, 2:PACK, :], op=ALU.mult
+                )
                 nc.sync.dma_start(out=out_cols(u), in_=scaled[u][:])
 
         def finish_first(u):
@@ -222,19 +231,17 @@ def tile_gdn_kernel(tc, x, beta, gamma, out):
                 nc.sync.dma_start(out=out_cols(u), in_=scaled[u][:])
 
         for u in range(UNITS):
-            ahead = u + LEAD
             banks = passes(u)
+            if HEAD_UNITS <= u + 1 < UNITS:
+                square_scalar(u + 1, 0, SCALAR_COLS)
             inverse_roots(u, banks)
-            if HEAD_UNITS <= ahead < UNITS:
-                square_scalar(ahead, 0, SCALAR_COLS)
-                square_vector(ahead, SCALAR_COLS, UNIT)
-            if u == 0:
-                quantise(HEAD_UNITS - 1)
-            if HEAD_UNITS <= ahead - 1 < UNITS:
-                quantise(ahead - 1)
+            if VECTOR_HEAD_UNITS <= u + 2 < UNITS:
+                square_vector(u + 2, SCALAR_COLS, UNIT)
+            if HEAD_UNITS <= u + 1 < UNITS:
+                quantise(u + 1)
             if u == 0:
                 finish_first(u)
             elif FIRST_ASSISTED <= u <= LAST_ASSISTED:
                 finish_assisted(u)
             else:
-                finish_by_rows(u, u == UNITS - 1)
+                finish_by_rows(u, True)

@@ -89,8 +89,8 @@ def tile_gdn_kernel(tc, x, beta, gamma, out):
 
         def square_views(u, c0, c1):
             return (
-                grouped_tile(u)[:, c0:c1, :].rearrange("p (c i) t -> p c t i", i=4),
-                x_cols(u, c0, c1).rearrange("p t (c i) -> p c t i", i=4),
+                grouped_tile(u)[:, c0:c1, :].rearrange("p (c i) t -> p c t i", i=8),
+                x_cols(u, c0, c1).rearrange("p t (c i) -> p c t i", i=8),
             )
 
         def square_scalar(u, c0, c1):

@@ -25,8 +25,8 @@ X_WIDTHS = (256, 256, 512, 512, 512, 512, 512, 1024, 2048, 2048)
 GAMMA_AFTER = 5
 BETA_AFTER = 6
 
-HEAD_UNITS = 5
-VECTOR_HEAD_UNITS = 7
+HEAD_UNITS = 6
+VECTOR_HEAD_UNITS = 8
 SCALAR_COLS = 280
 HEAD_SCALAR_COLS = 336
 FIRST_PIECE = 256
@@ -140,21 +140,25 @@ def tile_gdn_kernel(tc, x, beta, gamma, out):
         for c0 in (0, FIRST_PIECE):
             square_scalar(0, c0, c0 + FIRST_SCALAR_COLS)
             square_vector(0, c0 + FIRST_SCALAR_COLS, c0 + FIRST_PIECE)
-        for u in range(1, HEAD_UNITS - 1):
+        for u in range(1, HEAD_UNITS - 2):
             square_scalar(u, 0, HEAD_SCALAR_COLS)
             square_vector(u, HEAD_SCALAR_COLS, UNIT)
             quantise(u - 1)
         gamma_copy(nc.vector.tensor_copy, 0)
+        square_scalar(HEAD_UNITS - 2, 0, HEAD_SCALAR_COLS)
         square_scalar(HEAD_UNITS - 1, 0, HEAD_SCALAR_COLS)
         gamma_copy(nc.scalar.copy, 1)
-        quantise(HEAD_UNITS - 2)
+        quantise(HEAD_UNITS - 3)
         gamma_quantise(0)
-        square_vector(HEAD_UNITS - 1, HEAD_SCALAR_COLS, UNIT)
+        square_vector(HEAD_UNITS - 2, HEAD_SCALAR_COLS, UNIT)
         beta_f = keep.tile([P, PACK], F32, name="beta_f")
         nc.vector.tensor_copy(out=beta_f[:], in_=beta_bf[:])
+        square_vector(HEAD_UNITS - 1, HEAD_SCALAR_COLS, UNIT)
+        quantise(HEAD_UNITS - 2)
         gamma_quantise(1)
+        square_vector(HEAD_UNITS, SCALAR_COLS, UNIT)
         quantise(HEAD_UNITS - 1)
-        for u in range(HEAD_UNITS, VECTOR_HEAD_UNITS):
+        for u in range(HEAD_UNITS + 1, VECTOR_HEAD_UNITS):
             square_vector(u, SCALAR_COLS, UNIT)
 
         scaled = {}

@@ -27,10 +27,10 @@ BETA_AFTER = 6
 
 HEAD_UNITS = 6
 VECTOR_HEAD_UNITS = 8
-SCALAR_COLS = 280
-HEAD_SCALAR_COLS = 336
+SCALAR_COLS = 272
+HEAD_SCALAR_COLS = 320
 FIRST_PIECE = 256
-FIRST_SCALAR_COLS = 168
+FIRST_SCALAR_COLS = 160
 FIRST_ASSISTED = 1
 LAST_ASSISTED = 12
 VECTOR_COLS = 320

from contextlib import ExitStack

import concourse.mybir as mybir
from concourse.masks import make_identity

F32 = mybir.dt.float32
BF16 = mybir.dt.bfloat16
U32 = mybir.dt.uint32
U8 = mybir.dt.uint8
FP8X4 = mybir.dt.float8_e4m3fn_x4
ACT = mybir.ActivationFunctionType
ALU = mybir.AluOpType

P = 128
PACK = 4
BATCH = 2
CHANNELS = 512
PIXELS = 4096
UNIT = 512
UNITS = BATCH * PIXELS // UNIT

FLOPS = 2 * CHANNELS * CHANNELS * BATCH * PIXELS

X_WIDTHS = (256, 256, 512, 512, 512, 512, 512, 1024, 2048, 2048)
GAMMA_AFTER = 5
BETA_AFTER = 6

HEAD_UNITS = 6
VECTOR_HEAD_UNITS = 8
SCALAR_COLS = 272
HEAD_SCALAR_COLS = 320
FIRST_PIECE = 256
FIRST_SCALAR_COLS = 160
FIRST_ASSISTED = 1
LAST_ASSISTED = 12
VECTOR_COLS = 320


def tile_gdn_kernel(tc, x, beta, gamma, out):
    nc = tc.nc
    x_view = [x[b].rearrange("(p t) h w -> p t (h w)", t=PACK) for b in range(BATCH)]
    out_view = [out[b].rearrange("(p t) h w -> p t (h w)", t=PACK) for b in range(BATCH)]

    with ExitStack() as ctx:
        keep = ctx.enter_context(tc.tile_pool(name="keep", bufs=1))
        stage = ctx.enter_context(tc.tile_pool(name="stage", bufs=4))
        result = ctx.enter_context(tc.tile_pool(name="result", bufs=8))
        psum = ctx.enter_context(tc.psum_pool(name="psum", bufs=6))
        ctx.enter_context(tc.manual_schedule())

        gamma_rows = keep.tile([P, PACK * CHANNELS], BF16, name="gamma_rows")
        beta_bf = keep.tile([P, PACK], BF16, name="beta_bf")
        x_tiles = []
        start = 0
        for i, width in enumerate(X_WIDTHS):
            if i == GAMMA_AFTER:
                nc.sync.dma_start(out=gamma_rows[:], in_=gamma.rearrange("(m j) i a b -> m (j i a b)", j=PACK))
            if i == BETA_AFTER:
                nc.sync.dma_start(out=beta_bf[:], in_=beta.rearrange("a (p j) b c -> p (a j b c)", j=PACK))
            x_tile = keep.tile([P, PACK, width], BF16, name="x_tile%d" % i)
            first = start % PIXELS
            nc.sync.dma_start(out=x_tile[:], in_=x_view[start // PIXELS][:, :, first : first + width])
            x_tiles.append((start, width, x_tile))
            start += width

        ident = keep.tile([P, P], F32, name="ident")
        make_identity(nc, ident[:])
        ident_bf = keep.tile([P, P], BF16, name="ident_bf")
        make_identity(nc, ident_bf[:])
        one = keep.tile([P, 1], F32, name="one")
        nc.vector.memset(one[:], 1.0)
        warm = keep.tile([P, 1], F32, name="warm")
        nc.scalar.activation(out=warm[:], in_=one[:], func=ACT.Abs_reciprocal_sqrt)

        codes = [keep.tile([P, UNIT], U32, name="codes%d" % u, align_bytes=64) for u in range(UNITS)]
        scales = [keep.tile([P, UNIT], U8, name="scales%d" % u, align_bytes=64) for u in range(UNITS)]
        grouped = {}

        def grouped_tile(u):
            if u not in grouped:
                grouped[u] = stage.tile([P, UNIT, PACK], BF16, name="grouped", align_bytes=64)
            return grouped[u]

        def x_cols(u, c0, c1):
            for first, width, x_tile in x_tiles:
                if first <= u * UNIT + c0 and u * UNIT + c1 <= first + width:
                    return x_tile[:, :, u * UNIT + c0 - first : u * UNIT + c1 - first]
            raise ValueError("columns in two tiles")

        def square_views(u, c0, c1):
            return (
                grouped_tile(u)[:, c0:c1, :].rearrange("p (c i) t -> p c t i", i=8),
                x_cols(u, c0, c1).rearrange("p t (c i) -> p c t i", i=8),
            )

        def square_scalar(u, c0, c1):
            dst, src = square_views(u, c0, c1)
            nc.scalar.activation(out=dst, in_=src, func=ACT.Square)

        def square_vector(u, c0, c1):
            dst, src = square_views(u, c0, c1)
            nc.vector.tensor_tensor(out=dst, in0=src, in1=src, op=ALU.mult)

        def quantise(u):
            nc.vector.quantize_mx(
                out=codes[u][:].bitcast(FP8X4),
                scales=scales[u][:],
                in_=grouped[u][:].rearrange("p w t -> p (w t)"),
            )

        gamma_words = gamma_rows[:].bitcast(F32).rearrange("m (j q u) -> m j q u", j=PACK, u=2)
        gamma_grouped = keep.tile([P, PACK * P * PACK], BF16, name="gamma_grouped", align_bytes=64)
        gamma_grouped_words = gamma_grouped[:].bitcast(F32)
        gamma_codes = keep.tile([P, PACK * P], U32, name="gamma_codes", align_bytes=64)
        gamma_scales = keep.tile([P, PACK * P], U8, name="gamma_scales", align_bytes=64)
        gamma_banks = []
        for pair in range(2):
            bank = psum.tile([P, UNIT], F32, name="bank")
            for jj in range(2):
                for u in range(2):
                    col = (2 * jj + u) * P
                    nc.tensor.transpose(bank[:, col : col + P], gamma_words[:, 2 * pair + jj, :, u], ident[:])
            gamma_banks.append(bank)

        def gamma_copy(copy, pair):
            copy(
                out=gamma_grouped_words[:, pair * UNIT : (pair + 1) * UNIT].rearrange(
                    "q (jj m u) -> q jj m u", jj=2, u=2
                ),
                in_=gamma_banks[pair][:].rearrange("q (jj u m) -> q jj m u", jj=2, u=2),
            )

        def gamma_quantise(pair):
            nc.vector.quantize_mx(
                out=gamma_codes[:, pair * 2 * P : (pair + 1) * 2 * P].bitcast(FP8X4),
                scales=gamma_scales[:, pair * 2 * P : (pair + 1) * 2 * P],
                in_=gamma_grouped[:, pair * 2 * P * PACK : (pair + 1) * 2 * P * PACK],
            )

        for c0 in (0, FIRST_PIECE):
            square_scalar(0, c0, c0 + FIRST_SCALAR_COLS)
            square_vector(0, c0 + FIRST_SCALAR_COLS, c0 + FIRST_PIECE)
        for u in range(1, HEAD_UNITS - 2):
            square_scalar(u, 0, HEAD_SCALAR_COLS)
            square_vector(u, HEAD_SCALAR_COLS, UNIT)
            quantise(u - 1)
        gamma_copy(nc.vector.tensor_copy, 0)
        square_scalar(HEAD_UNITS - 2, 0, HEAD_SCALAR_COLS)
        square_scalar(HEAD_UNITS - 1, 0, HEAD_SCALAR_COLS)
        gamma_copy(nc.scalar.copy, 1)
        quantise(HEAD_UNITS - 3)
        gamma_quantise(0)
        square_vector(HEAD_UNITS - 2, HEAD_SCALAR_COLS, UNIT)
        beta_f = keep.tile([P, PACK], F32, name="beta_f")
        nc.vector.tensor_copy(out=beta_f[:], in_=beta_bf[:])
        square_vector(HEAD_UNITS - 1, HEAD_SCALAR_COLS, UNIT)
        quantise(HEAD_UNITS - 2)
        gamma_quantise(1)
        square_vector(HEAD_UNITS, SCALAR_COLS, UNIT)
        quantise(HEAD_UNITS - 1)
        for u in range(HEAD_UNITS + 1, VECTOR_HEAD_UNITS):
            square_vector(u, SCALAR_COLS, UNIT)

        scaled = {}
        x_banks = {}

        def out_cols(u):
            return out_view[u // 8][:, :, (u % 8) * UNIT : (u % 8 + 1) * UNIT]

        def passes(u):
            banks = []
            for j in range(PACK):
                bank = psum.tile([P, UNIT], F32, name="bank")
                nc.tensor.matmul_mx(
                    out=bank[:],
                    lhsT=gamma_codes[:, j * P : (j + 1) * P].bitcast(FP8X4),
                    lhsT_scale=gamma_scales[:, j * P : (j + 1) * P],
                    rhs=codes[u][:].bitcast(FP8X4),
                    rhs_scale=scales[u][:],
                    start=True,
                    stop=True,
                )
                banks.append(bank)
            if FIRST_ASSISTED <= u <= LAST_ASSISTED:
                x_banks[u] = psum.tile([P, 2, UNIT], BF16, name="x_bank", bufs=2)
                for j in range(2):
                    nc.tensor.matmul(
                        out=x_banks[u][:, j, :], lhsT=ident_bf[:], rhs=x_cols(u, 0, UNIT)[:, 2 + j, :], start=True, stop=True
                    )
            return banks

        def inverse_roots(u, banks):
            scaled[u] = result.tile([P, PACK, UNIT], F32, name="scaled")
            for j in range(PACK):
                nc.scalar.activation(
                    out=scaled[u][:, j, :],
                    in_=banks[j][:],
                    func=ACT.Abs_reciprocal_sqrt,
                    bias=beta_f[:, j : j + 1],
                    scale=1.0,
                )

        def finish_assisted(u):
            part = scaled[u][:, 0:2, 0:VECTOR_COLS]
            nc.vector.tensor_tensor(out=part, in0=part, in1=x_cols(u, 0, VECTOR_COLS)[:, 0:2, :], op=ALU.mult)
            rest = scaled[u][:, 0:2, VECTOR_COLS:UNIT]
            nc.gpsimd.tensor_tensor(out=rest, in0=rest, in1=x_cols(u, VECTOR_COLS, UNIT)[:, 0:2, :], op=ALU.mult)
            if u == LAST_ASSISTED:
                for j in range(2, PACK):
                    nc.vector.tensor_tensor(
                        out=scaled[u][:, j, :], in0=x_banks[u][:, j - 2, :], in1=scaled[u][:, j, :], op=ALU.mult
                    )
                    nc.sync.dma_start(out=out_cols(u)[:, j, :], in_=scaled[u][:, j, :])
                nc.sync.dma_start(out=out_cols(u)[:, 0:2, :], in_=scaled[u][:, 0:2, :])
            else:
                nc.vector.tensor_tensor(
                    out=scaled[u][:, 2:PACK, :], in0=x_banks[u][:], in1=scaled[u][:, 2:PACK, :], op=ALU.mult
                )
                nc.sync.dma_start(out=out_cols(u), in_=scaled[u][:])

        def finish_first(u):
            for c0 in (0, FIRST_PIECE):
                piece = scaled[u][:, :, c0 : c0 + FIRST_PIECE]
                nc.vector.tensor_tensor(out=piece, in0=piece, in1=x_cols(u, c0, c0 + FIRST_PIECE), op=ALU.mult)
            nc.sync.dma_start(out=out_cols(u), in_=scaled[u][:])

        def finish_by_rows(u, store_rows):
            for j in range(PACK):
                nc.vector.tensor_tensor(
                    out=scaled[u][:, j, :], in0=scaled[u][:, j, :], in1=x_cols(u, 0, UNIT)[:, j, :], op=ALU.mult
                )
                if store_rows:
                    nc.sync.dma_start(out=out_cols(u)[:, j, :], in_=scaled[u][:, j, :])
            if not store_rows:
                nc.sync.dma_start(out=out_cols(u), in_=scaled[u][:])

        for u in range(UNITS):
            banks = passes(u)
            if HEAD_UNITS <= u + 1 < UNITS:
                square_scalar(u + 1, 0, SCALAR_COLS)
            inverse_roots(u, banks)
            if VECTOR_HEAD_UNITS <= u + 2 < UNITS:
                square_vector(u + 2, SCALAR_COLS, UNIT)
            if HEAD_UNITS <= u + 1 < UNITS:
                quantise(u + 1)
            if u == 0:
                finish_first(u)
            elif FIRST_ASSISTED <= u <= LAST_ASSISTED:
                finish_assisted(u)
            else:
                finish_by_rows(u, True)
